import numpy as np
import ml_dtypes


def mxq(x, axis, fmt="e4m3"):
    dtype, down = {"e4m3": (ml_dtypes.float8_e4m3fn, 7), "e5m2": (ml_dtypes.float8_e5m2, 14)}[fmt]
    v = np.moveaxis(np.asarray(x, np.float32).astype(ml_dtypes.bfloat16).astype(np.float64), axis, -1)
    blocks = v.reshape(v.shape[:-1] + (-1, 32))
    amax = np.abs(blocks).max(-1, keepdims=True)
    byte = np.maximum(np.where(amax > 0, np.frexp(amax)[1] - 1 + 127, 0) - down, 1)
    scale = np.exp2(byte - 127.0)
    codes = (blocks / scale).astype(np.float32).astype(dtype).astype(np.float64)
    return np.moveaxis((codes * scale).reshape(v.shape), -1, axis)


WIDE = False


def mx_kscale(k):
    if not WIDE:
        return np.ones(k)
    levels = np.array([10, -10, 5, -5, 0])
    a = np.random.permutation(np.resize(levels, k // 512 * 4)).reshape(k // 512, 4)
    idx = np.arange(k)
    return np.exp2(a[idx // 512, idx % 128 // 32])


BF16 = ml_dtypes.bfloat16


def bf(x):
    return np.asarray(x, np.float32).astype(BF16)


def f64(x):
    return np.asarray(x).astype(np.float64)


E2M1 = np.array([0.0, 0.5, 1.0, 1.5, 2.0, 3.0, 4.0, 6.0, -0.0, -0.5, -1.0, -1.5, -2.0, -3.0, -4.0, -6.0])


def pack_weight(w, fmt):
    k, n = w.shape
    w = f64(bf(w)).reshape(k // 32, 32, n)
    amax = np.abs(w).max(1)
    if fmt == "e4m3":
        byte = np.frexp(amax)[1] - 1 + 127 - 7
    else:
        mant, ex = np.frexp(amax / 6.0)
        byte = np.where(mant > 0.5, ex, ex - 1) + 127
    byte = np.clip(np.where(amax > 0, byte, 1), 1, 254)
    scaled = (w * np.exp2(127.0 - byte)[:, None, :]).reshape(k, n).astype(np.float32)
    by_word = np.ascontiguousarray(scaled.reshape(k // 512, 128, 4, n).transpose(0, 1, 3, 2))
    if fmt == "e4m3":
        words = by_word.astype(ml_dtypes.float8_e4m3fn).view(np.uint8)
    else:
        c = by_word.astype(ml_dtypes.float4_e2m1fn).view(np.uint8) & 0xF
        words = c[..., 0::2] | (c[..., 1::2] << 4)
    return np.ascontiguousarray(words), np.ascontiguousarray(byte.astype(np.uint8).reshape(k // 512, 16, n))


def unpack_weight(words, scales, fmt):
    g, p, n, _ = words.shape
    if fmt == "e4m3":
        vals = np.ascontiguousarray(words).view(ml_dtypes.float8_e4m3fn).astype(np.float64)
    else:
        nib = np.empty((g, p, n, 4), np.uint8)
        nib[..., 0::2] = words & 0xF
        nib[..., 1::2] = words >> 4
        vals = E2M1[nib]
    vals = vals * np.repeat(np.exp2(scales.astype(np.float64) - 127.0), 8, axis=1)[..., None]
    return vals.transpose(0, 1, 3, 2).reshape(g * 512, n)


B, IN, HID, N, NM = 8, 384, 128, 512, 5
C = IN + HID
K = NM * C


def setup_inputs():
    t = mx_kscale(C)
    tc = t[None, :, None]
    x_cand = bf(np.random.standard_normal((B, C, N)) * 0.8 * tc)
    x1_0 = bf(np.random.standard_normal((B, C, N)) * 0.55 * tc)
    x1_1 = bf(np.random.standard_normal((B, C, N)) * 0.55 * tc)
    support0 = bf(np.random.standard_normal((N, N)) * 0.7 / np.sqrt(N))
    support1 = bf(np.random.standard_normal((N, N)) * 0.7 / np.sqrt(N))
    words, scales = pack_weight(np.random.standard_normal((K, HID)) / np.sqrt(K) / np.tile(t, NM)[:, None], "e4m3")
    b_c = bf(0.3 * np.random.standard_normal(HID))
    u = bf(1.0 / (1.0 + np.exp(-(1.0 + np.random.standard_normal((B, HID, N))))))
    hx = bf(np.random.standard_normal((B, HID, N)))
    return {"x_cand": x_cand,
            "x1_0": x1_0,
            "x1_1": x1_1,
            "support0": support0,
            "support1": support1,
            "W_c_words": words,
            "W_c_scales": scales,
            "b_c": b_c,
            "u": u,
            "hx": hx}


def reference(x_cand, x1_0, x1_1, support0, support1, W_c_words, W_c_scales, b_c, u, hx):
    x0, xa, xb = f64(x_cand), f64(x1_0), f64(x1_1)
    x2a = 2.0 * (mxq(xa, 2, "e4m3") @ mxq(f64(support0).T, 0, "e4m3")) - x0
    x2b = 2.0 * (mxq(xb, 2, "e4m3") @ mxq(f64(support1).T, 0, "e4m3")) - x0
    h = np.concatenate([x0, xa, x2a, xb, x2b], axis=1)
    cand = np.tanh((unpack_weight(W_c_words, W_c_scales, "e4m3").T @ mxq(h, 1, "e4m3")) + f64(b_c)[None, :, None])
    return f64(u) * f64(hx) + (1.0 - f64(u)) * cand

@@ -1,0 +1,292 @@
+from contextlib import ExitStack
+
+import concourse.mybir as mybir
+from concourse.masks import make_identity
+
+F32 = mybir.dt.float32
+BF16 = mybir.dt.bfloat16
+I32 = mybir.dt.int32
+U32 = mybir.dt.uint32
+U8 = mybir.dt.uint8
+FP8X4 = mybir.dt.float8_e4m3fn_x4
+ALU = mybir.AluOpType
+TANH = mybir.ActivationFunctionType.Tanh
+
+P = 128
+PACK = 4
+BATCH = 8
+CHANNELS = 512
+NODES = 512
+GROUPS = 5
+HIDDEN = 128
+X1_NAMES = ("xa", "xb")
+
+FLOPS = 2 * 2 * BATCH * CHANNELS * NODES * NODES + 2 * BATCH * HIDDEN * NODES * GROUPS * CHANNELS
+
+
+def tile_dcgrucell_pc_t_kernel(
+    tc, x_cand, x1_0, x1_1, support0, support1, W_c_words, W_c_scales, b_c, u, hx, out
+):
+    nc = tc.nc
+    with ExitStack() as ctx:
+        consts = ctx.enter_context(tc.tile_pool(name="consts", bufs=1))
+        rows_pool = ctx.enter_context(tc.tile_pool(name="rows", bufs=3))
+        gates_pool = ctx.enter_context(tc.tile_pool(name="gates", bufs=4))
+        work = ctx.enter_context(tc.tile_pool(name="work", bufs=2))
+        flip_pool = ctx.enter_context(tc.psum_pool(name="flip", bufs=2))
+        diff_pool = ctx.enter_context(tc.psum_pool(name="diff", bufs=4))
+        mix_pool = ctx.enter_context(tc.psum_pool(name="mix", bufs=2))
+        ctx.enter_context(tc.manual_schedule())
+
+        x_sources = {"x0": x_cand, "xa": x1_0, "xb": x1_1}
+        gate_sources = {"u": u, "hx": hx}
+        loaded = {}
+        by_node = {}
+        flipped = {}
+        grouped = {}
+        h_mx = {}
+        banks = {}
+        mixed = {}
+        blend = {}
+
+        def load_rows(name, b):
+            rows = rows_pool.tile([P, PACK, NODES], BF16, name=name)
+            nc.sync.dma_start(
+                out=rows[:], in_=x_sources[name][b].rearrange("(p j) n -> p j n", j=PACK)
+            )
+            loaded[(name, b)] = rows
+
+        def load_gates(b):
+            for name in ("u", "hx"):
+                gate = gates_pool.tile([P, NODES], BF16, name=name)
+                nc.sync.dma_start(out=gate[:], in_=gate_sources[name][b])
+                loaded[(name, b)] = gate
+
+        def load_batch(b):
+            for name in ("xa", "xb", "x0"):
+                load_rows(name, b)
+            load_gates(b)
+
+        def nodes_to_partitions(rows, copy):
+            result = work.tile([P, PACK * P, PACK], BF16, name="by_node", align_bytes=64)
+            row_words = rows[:].bitcast(F32)
+            result_words = result[:].bitcast(F32)
+            for half in range(2):
+                bank = flip_pool.tile([P, 2, 2, P], F32, name="flip_bank")
+                for r in range(2):
+                    for v in range(2):
+                        nc.tensor.transpose(
+                            bank[:, r, v, :],
+                            row_words[:, 2 * half + r, v * P : (v + 1) * P],
+                            identity[:],
+                        )
+                copy(
+                    out=result_words[:, 2 * P * half : 2 * P * (half + 1), :].rearrange(
+                        "q (r c) v -> q r c v", r=2
+                    ),
+                    in_=bank[:].rearrange("q r v c -> q r c v"),
+                )
+            return result
+
+        def quantise(values, codes, scales):
+            nc.vector.quantize_mx(
+                out=codes.bitcast(FP8X4),
+                scales=scales,
+                in_=values[:].rearrange("p c t -> p (c t)"),
+            )
+
+        def flip(b, s):
+            by_node[(b, s)] = nodes_to_partitions(loaded[(X1_NAMES[s], b)], nc.scalar.copy)
+
+        def quantise_flipped(b, s):
+            codes = work.tile([P, CHANNELS], U32, name="flip_codes%d" % s, align_bytes=64)
+            scales = work.tile([P, CHANNELS], U8, name="flip_scales%d" % s, align_bytes=64)
+            quantise(by_node[(b, s)], codes[:], scales[:])
+            flipped[(b, s)] = (codes, scales)
+
+        def regroup(name, group, b, copy):
+            by_channel = work.tile([P, NODES, PACK], BF16, name="h%d" % group, align_bytes=64)
+            copy(
+                out=by_channel[:].rearrange("p (c i) j -> p c j i", i=4),
+                in_=loaded[(name, b)][:].rearrange("p j (c i) -> p c j i", i=4),
+            )
+            grouped[(group, b)] = by_channel
+
+        def diffuse(b, s):
+            codes, scales = flipped[(b, s)]
+            support_codes, support_scales = support_mx[s]
+            banks[(b, s)] = []
+            for m in range(NODES // P):
+                bank = diff_pool.tile([P, PACK, P], F32, name="diff_bank")
+                for j in range(PACK):
+                    nc.tensor.matmul_mx(
+                        out=bank[:, j, :],
+                        lhsT=codes[:, j * P : (j + 1) * P].bitcast(FP8X4),
+                        lhsT_scale=scales[:, j * P : (j + 1) * P],
+                        rhs=support_codes[:, m * P : (m + 1) * P].bitcast(FP8X4),
+                        rhs_scale=support_scales[:, m * P : (m + 1) * P],
+                        start=True,
+                        stop=True,
+                    )
+                banks[(b, s)].append(bank)
+
+        def finish_x2(b, s):
+            group = 2 + 2 * s
+            x2 = work.tile([P, NODES, PACK], BF16, name="h%d" % group, align_bytes=64)
+            for m, bank in enumerate(banks[(b, s)]):
+                nc.vector.scalar_tensor_tensor(
+                    out=x2[:, m * P : (m + 1) * P, :],
+                    in0=bank[:].rearrange("p j m -> p m j"),
+                    scalar=2.0,
+                    in1=grouped[(0, b)][:, m * P : (m + 1) * P, :],
+                    op0=ALU.mult,
+                    op1=ALU.subtract,
+                )
+            grouped[(group, b)] = x2
+
+        def open_mix(b):
+            h_codes = work.tile([P, GROUPS, NODES], U32, name="h_codes", align_bytes=64)
+            h_scales = work.tile([P, GROUPS, NODES], U8, name="h_scales", align_bytes=64)
+            h_mx[b] = (h_codes, h_scales)
+            mixed[b] = mix_pool.tile([P, NODES], F32, name="mix_bank")
+
+        def mix_groups(b, groups):
+            h_codes, h_scales = h_mx[b]
+            for g in groups:
+                quantise(grouped[(g, b)], h_codes[:, g, :], h_scales[:, g, :])
+            for g in groups:
+                nc.tensor.matmul_mx(
+                    out=mixed[b][:],
+                    lhsT=w_words[:, g, :].bitcast(FP8X4),
+                    lhsT_scale=w_scales[:, g, :],
+                    rhs=h_codes[:, g, :].bitcast(FP8X4),
+                    rhs_scale=h_scales[:, g, :],
+                    start=(g == 0),
+                    stop=(g == GROUPS - 1),
+                )
+
+        def candidate(b):
+            cand = work.tile([P, NODES], F32, name="cand")
+            nc.scalar.activation(out=cand[:], in_=mixed[b][:], func=TANH, bias=bias[:, 0:1], scale=1.0)
+            blend[("cand", b)] = cand
+
+        def keep_old_state(b):
+            kept = work.tile([P, NODES], F32, name="kept")
+            nc.vector.tensor_tensor(
+                out=kept[:], in0=loaded[("u", b)][:], in1=loaded[("hx", b)][:], op=ALU.mult
+            )
+            blend[("kept", b)] = kept
+
+        def weigh_candidate(b):
+            weighed = work.tile([P, NODES], F32, name="weighed")
+            nc.vector.scalar_tensor_tensor(
+                out=weighed[:],
+                in0=loaded[("u", b)][:],
+                scalar=1.0,
+                in1=blend[("cand", b)][:],
+                op0=ALU.subtract,
+                op1=ALU.mult,
+            )
+            blend[("weighed", b)] = weighed
+
+        def store_state(b):
+            state = work.tile([P, NODES], F32, name="state")
+            nc.vector.tensor_tensor(
+                out=state[:], in0=blend[("kept", b)][:], in1=blend[("weighed", b)][:], op=ALU.subtract
+            )
+            nc.sync.dma_start(out=out[b], in_=state[:])
+
+        identity = consts.tile([P, P], F32, name="identity")
+        make_identity(nc, identity[:])
+        w_words = consts.tile([P, GROUPS, HIDDEN], U32, name="w_words", align_bytes=64)
+        w_scales = consts.tile([P, GROUPS, HIDDEN], U8, name="w_scales", align_bytes=64)
+        nc.vector.memset(w_scales[:].bitcast(I32), 0)
+        bias_rows = consts.tile([P, P], BF16, name="bias_rows")
+        nc.vector.memset(bias_rows[:], 0.0)
+        nc.scalar.dma_start(out=bias_rows[0:1, :], in_=b_c.rearrange("(o h) -> o h", o=1))
+
+        support_rows = []
+        for s in range(2):
+            support_rows.append(consts.tile([P, PACK, NODES], BF16, name="support_rows%d" % s))
+
+        def load_support(s, support):
+            nc.sync.dma_start(
+                out=support_rows[s][:], in_=support.rearrange("(r p) n -> p r n", p=P)
+            )
+
+        load_rows("xa", 0)
+        load_support(0, support0)
+        load_rows("x0", 0)
+        load_rows("xb", 0)
+        load_support(1, support1)
+        nc.sync.dma_start(
+            out=w_words[:].bitcast(I32),
+            in_=W_c_words.rearrange("g p n t -> p g (n t)").bitcast(I32),
+        )
+        scale_rows = W_c_scales.rearrange("g (q r) n -> r q g n", r=4)
+        for r in range(4):
+            nc.sync.dma_start(
+                out=w_scales[r:P:32].bitcast(I32), in_=scale_rows[r].bitcast(I32)
+            )
+        load_gates(0)
+        load_batch(1)
+
+        bias_rows_f32 = consts.tile([P, P], F32, name="bias_rows_f32")
+        nc.vector.tensor_copy(out=bias_rows_f32[:], in_=bias_rows[:])
+        bias_bank = flip_pool.tile([P, 2, 2, P], F32, name="flip_bank")
+        nc.tensor.transpose(bias_bank[:, 0, 0, :], bias_rows_f32[:], identity[:])
+        bias = consts.tile([P, 1], F32, name="bias")
+        nc.vector.tensor_copy(out=bias[:], in_=bias_bank[:, 0, 0, 0:1])
+
+        support_mx = {}
+
+        def prepare_support(s):
+            flipped_support = nodes_to_partitions(support_rows[s], nc.vector.tensor_copy)
+            codes = consts.tile([P, NODES], U32, name="support_codes%d" % s, align_bytes=64)
+            scales = consts.tile([P, NODES], U8, name="support_scales%d" % s, align_bytes=64)
+            quantise(flipped_support, codes[:], scales[:])
+            support_mx[s] = (codes, scales)
+
+        flip(0, 0)
+        prepare_support(0)
+        quantise_flipped(0, 0)
+        diffuse(0, 0)
+        regroup("x0", 0, 0, nc.vector.tensor_copy)
+        regroup("xa", 1, 0, nc.scalar.copy)
+        finish_x2(0, 0)
+        flip(0, 1)
+        prepare_support(1)
+        quantise_flipped(0, 1)
+        regroup("xb", 3, 0, nc.scalar.copy)
+
+        for b in range(BATCH):
+            if b + 2 < BATCH:
+                load_batch(b + 2)
+            if b > 0:
+                candidate(b - 1)
+            diffuse(b, 1)
+            if b + 1 < BATCH:
+                regroup("x0", 0, b + 1, nc.scalar.copy)
+                flip(b + 1, 0)
+                flip(b + 1, 1)
+                regroup("xa", 1, b + 1, nc.scalar.copy)
+                regroup("xb", 3, b + 1, nc.scalar.copy)
+            open_mix(b)
+            mix_groups(b, (0, 1))
+            if b > 0:
+                weigh_candidate(b - 1)
+            keep_old_state(b)
+            if b > 0:
+                store_state(b - 1)
+            finish_x2(b, 1)
+            mix_groups(b, (2, 3))
+            if b + 1 < BATCH:
+                quantise_flipped(b + 1, 0)
+                quantise_flipped(b + 1, 1)
+                diffuse(b + 1, 0)
+            mix_groups(b, (4,))
+            if b + 1 < BATCH:
+                finish_x2(b + 1, 0)
+        candidate(BATCH - 1)
+        weigh_candidate(BATCH - 1)
+        store_state(BATCH - 1)

@@ -172,7 +172,7 @@ def tile_dcgrucell_pc_t_kernel(
 
         def keep_old_state(b):
             kept = work.tile([P, NODES], F32, name="kept")
-            nc.vector.tensor_tensor(
+            nc.gpsimd.tensor_tensor(
                 out=kept[:], in0=loaded[("u", b)][:], in1=loaded[("hx", b)][:], op=ALU.mult
             )
             blend[("kept", b)] = kept
@@ -189,9 +189,9 @@ def tile_dcgrucell_pc_t_kernel(
             )
             blend[("weighed", b)] = weighed
 
-        def store_state(b):
+        def store_state(b, engine):
             state = work.tile([P, NODES], F32, name="state")
-            nc.vector.tensor_tensor(
+            engine.tensor_tensor(
                 out=state[:], in0=blend[("kept", b)][:], in1=blend[("weighed", b)][:], op=ALU.subtract
             )
             nc.sync.dma_start(out=out[b], in_=state[:])
@@ -200,10 +200,9 @@ def tile_dcgrucell_pc_t_kernel(
         make_identity(nc, identity[:])
         w_words = consts.tile([P, GROUPS, HIDDEN], U32, name="w_words", align_bytes=64)
         w_scales = consts.tile([P, GROUPS, HIDDEN], U8, name="w_scales", align_bytes=64)
-        nc.vector.memset(w_scales[:].bitcast(I32), 0)
         bias_rows = consts.tile([P, P], BF16, name="bias_rows")
         nc.vector.memset(bias_rows[:], 0.0)
-        nc.scalar.dma_start(out=bias_rows[0:1, :], in_=b_c.rearrange("(o h) -> o h", o=1))
+        nc.vector.memset(w_scales[:].bitcast(I32), 0)
 
         support_rows = []
         for s in range(2):
@@ -214,6 +213,7 @@ def tile_dcgrucell_pc_t_kernel(
                 out=support_rows[s][:], in_=support.rearrange("(r p) n -> p r n", p=P)
             )
 
+        nc.sync.dma_start(out=bias_rows[0:1, :], in_=b_c.rearrange("(o h) -> o h", o=1))
         load_rows("xa", 0)
         load_support(0, support0)
         load_rows("x0", 0)
@@ -275,9 +275,8 @@ def tile_dcgrucell_pc_t_kernel(
             mix_groups(b, (0, 1))
             if b > 0:
                 weigh_candidate(b - 1)
+                store_state(b - 1, nc.gpsimd)
             keep_old_state(b)
-            if b > 0:
-                store_state(b - 1)
             finish_x2(b, 1)
             mix_groups(b, (2, 3))
             if b + 1 < BATCH:
@@ -289,4 +288,4 @@ def tile_dcgrucell_pc_t_kernel(
                 finish_x2(b + 1, 0)
         candidate(BATCH - 1)
         weigh_candidate(BATCH - 1)
-        store_state(BATCH - 1)
+        store_state(BATCH - 1, nc.vector)

@@ -19,6 +19,9 @@ CHANNELS = 512
 NODES = 512
 GROUPS = 5
 HIDDEN = 128
+ALL_NODES = slice(0, NODES)
+GPSIMD_NODES = slice(0, NODES // 2)
+SCALAR_NODES = slice(NODES // 2, NODES)
 X1_NAMES = ("xa", "xb")
 
 FLOPS = 2 * 2 * BATCH * CHANNELS * NODES * NODES + 2 * BATCH * HIDDEN * NODES * GROUPS * CHANNELS
@@ -104,13 +107,28 @@ def tile_dcgrucell_pc_t_kernel(
             quantise(by_node[(b, s)], codes[:], scales[:])
             flipped[(b, s)] = (codes, scales)
 
-        def regroup(name, group, b, copy):
-            by_channel = work.tile([P, NODES, PACK], BF16, name="h%d" % group, align_bytes=64)
+        def group_tile(group, b):
+            if (group, b) not in grouped:
+                grouped[(group, b)] = work.tile(
+                    [P, NODES, PACK], BF16, name="h%d" % group, align_bytes=64
+                )
+            return grouped[(group, b)]
+
+        def regroup(name, group, b, copy, nodes):
             copy(
-                out=by_channel[:].rearrange("p (c i) j -> p c j i", i=4),
-                in_=loaded[(name, b)][:].rearrange("p j (c i) -> p c j i", i=4),
+                out=group_tile(group, b)[:, nodes, :].rearrange("p (c i) j -> p c j i", i=4),
+                in_=loaded[(name, b)][:, :, nodes].rearrange("p j (c i) -> p c j i", i=4),
             )
-            grouped[(group, b)] = by_channel
+
+        def regroup_on_gpsimd(name, group, b, nodes):
+            nc.gpsimd.tensor_scalar(
+                out=group_tile(group, b)[:, nodes, :],
+                in0=loaded[(name, b)][:, :, nodes].rearrange("p j n -> p n j"),
+                scalar1=1.0,
+                scalar2=0.0,
+                op0=ALU.mult,
+                op1=ALU.add,
+            )
 
         def diffuse(b, s):
             codes, scales = flipped[(b, s)]
@@ -131,8 +149,7 @@ def tile_dcgrucell_pc_t_kernel(
                 banks[(b, s)].append(bank)
 
         def finish_x2(b, s):
-            group = 2 + 2 * s
-            x2 = work.tile([P, NODES, PACK], BF16, name="h%d" % group, align_bytes=64)
+            x2 = group_tile(2 + 2 * s, b)
             for m, bank in enumerate(banks[(b, s)]):
                 nc.vector.scalar_tensor_tensor(
                     out=x2[:, m * P : (m + 1) * P, :],
@@ -142,7 +159,6 @@ def tile_dcgrucell_pc_t_kernel(
                     op0=ALU.mult,
                     op1=ALU.subtract,
                 )
-            grouped[(group, b)] = x2
 
         def open_mix(b):
             h_codes = work.tile([P, GROUPS, NODES], U32, name="h_codes", align_bytes=64)
@@ -251,40 +267,40 @@ def tile_dcgrucell_pc_t_kernel(
         prepare_support(0)
         quantise_flipped(0, 0)
         diffuse(0, 0)
-        regroup("x0", 0, 0, nc.vector.tensor_copy)
-        regroup("xa", 1, 0, nc.scalar.copy)
+        regroup("x0", 0, 0, nc.vector.tensor_copy, ALL_NODES)
+        regroup("xa", 1, 0, nc.scalar.copy, ALL_NODES)
         finish_x2(0, 0)
         flip(0, 1)
         prepare_support(1)
         quantise_flipped(0, 1)
-        regroup("xb", 3, 0, nc.scalar.copy)
+        regroup("xb", 3, 0, nc.scalar.copy, ALL_NODES)
 
         for b in range(BATCH):
             if b + 2 < BATCH:
                 load_batch(b + 2)
-            if b > 0:
-                candidate(b - 1)
             diffuse(b, 1)
             if b + 1 < BATCH:
-                regroup("x0", 0, b + 1, nc.scalar.copy)
                 flip(b + 1, 0)
                 flip(b + 1, 1)
-                regroup("xa", 1, b + 1, nc.scalar.copy)
-                regroup("xb", 3, b + 1, nc.scalar.copy)
-            open_mix(b)
-            mix_groups(b, (0, 1))
             if b > 0:
-                weigh_candidate(b - 1)
-                store_state(b - 1, nc.gpsimd)
-            keep_old_state(b)
+                candidate(b - 1)
+            if b + 1 < BATCH:
+                regroup("x0", 0, b + 1, nc.scalar.copy, ALL_NODES)
+                regroup("xa", 1, b + 1, nc.scalar.copy, ALL_NODES)
+                regroup("xb", 3, b + 1, nc.scalar.copy, SCALAR_NODES)
             finish_x2(b, 1)
-            mix_groups(b, (2, 3))
+            open_mix(b)
+            mix_groups(b, range(GROUPS))
             if b + 1 < BATCH:
                 quantise_flipped(b + 1, 0)
                 quantise_flipped(b + 1, 1)
                 diffuse(b + 1, 0)
-            mix_groups(b, (4,))
+            if b > 0:
+                weigh_candidate(b - 1)
+                store_state(b - 1, nc.gpsimd)
+            keep_old_state(b)
             if b + 1 < BATCH:
+                regroup_on_gpsimd("xb", 3, b + 1, GPSIMD_NODES)
                 finish_x2(b + 1, 0)
         candidate(BATCH - 1)
         weigh_candidate(BATCH - 1)

@@ -70,7 +70,7 @@ def tile_dcgrucell_pc_t_kernel(
                 load_rows(name, b)
             load_gates(b)
 
-        def nodes_to_partitions(rows, copy):
+        def nodes_to_partitions(rows):
             result = work.tile([P, PACK * P, PACK], BF16, name="by_node", align_bytes=64)
             row_words = rows[:].bitcast(F32)
             result_words = result[:].bitcast(F32)
@@ -83,7 +83,7 @@ def tile_dcgrucell_pc_t_kernel(
                             row_words[:, 2 * half + r, v * P : (v + 1) * P],
                             identity[:],
                         )
-                copy(
+                nc.scalar.copy(
                     out=result_words[:, 2 * P * half : 2 * P * (half + 1), :].rearrange(
                         "q (r c) v -> q r c v", r=2
                     ),
@@ -99,7 +99,7 @@ def tile_dcgrucell_pc_t_kernel(
             )
 
         def flip(b, s):
-            by_node[(b, s)] = nodes_to_partitions(loaded[(X1_NAMES[s], b)], nc.scalar.copy)
+            by_node[(b, s)] = nodes_to_partitions(loaded[(X1_NAMES[s], b)])
 
         def quantise_flipped(b, s):
             codes = work.tile([P, CHANNELS], U32, name="flip_codes%d" % s, align_bytes=64)
@@ -244,8 +244,10 @@ def tile_dcgrucell_pc_t_kernel(
             nc.sync.dma_start(
                 out=w_scales[r:P:32].bitcast(I32), in_=scale_rows[r].bitcast(I32)
             )
+        for name in ("xa", "xb", "x0"):
+            load_rows(name, 1)
         load_gates(0)
-        load_batch(1)
+        load_gates(1)
 
         bias_rows_f32 = consts.tile([P, P], F32, name="bias_rows_f32")
         nc.vector.tensor_copy(out=bias_rows_f32[:], in_=bias_rows[:])
@@ -254,25 +256,30 @@ def tile_dcgrucell_pc_t_kernel(
         bias = consts.tile([P, 1], F32, name="bias")
         nc.vector.tensor_copy(out=bias[:], in_=bias_bank[:, 0, 0, 0:1])
 
+        support_by_node = {}
         support_mx = {}
 
-        def prepare_support(s):
-            flipped_support = nodes_to_partitions(support_rows[s], nc.vector.tensor_copy)
+        def flip_support(s):
+            support_by_node[s] = nodes_to_partitions(support_rows[s])
+
+        def quantise_support(s):
             codes = consts.tile([P, NODES], U32, name="support_codes%d" % s, align_bytes=64)
             scales = consts.tile([P, NODES], U8, name="support_scales%d" % s, align_bytes=64)
-            quantise(flipped_support, codes[:], scales[:])
+            quantise(support_by_node[s], codes[:], scales[:])
             support_mx[s] = (codes, scales)
 
+        regroup("xa", 1, 0, nc.vector.tensor_copy, ALL_NODES)
         flip(0, 0)
-        prepare_support(0)
+        flip_support(0)
         quantise_flipped(0, 0)
-        diffuse(0, 0)
         regroup("x0", 0, 0, nc.vector.tensor_copy, ALL_NODES)
-        regroup("xa", 1, 0, nc.scalar.copy, ALL_NODES)
+        quantise_support(0)
+        diffuse(0, 0)
         finish_x2(0, 0)
         flip(0, 1)
-        prepare_support(1)
+        flip_support(1)
         quantise_flipped(0, 1)
+        quantise_support(1)
         regroup("xb", 3, 0, nc.scalar.copy, ALL_NODES)
 
         for b in range(BATCH):
@@ -280,12 +287,12 @@ def tile_dcgrucell_pc_t_kernel(
                 load_batch(b + 2)
             diffuse(b, 1)
             if b + 1 < BATCH:
+                regroup("x0", 0, b + 1, nc.scalar.copy, ALL_NODES)
                 flip(b + 1, 0)
                 flip(b + 1, 1)
             if b > 0:
                 candidate(b - 1)
             if b + 1 < BATCH:
-                regroup("x0", 0, b + 1, nc.scalar.copy, ALL_NODES)
                 regroup("xa", 1, b + 1, nc.scalar.copy, ALL_NODES)
                 regroup("xb", 3, b + 1, nc.scalar.copy, SCALAR_NODES)
             finish_x2(b, 1)

@@ -20,8 +20,10 @@ NODES = 512
 GROUPS = 5
 HIDDEN = 128
 ALL_NODES = slice(0, NODES)
-GPSIMD_NODES = slice(0, NODES // 2)
-SCALAR_NODES = slice(NODES // 2, NODES)
+GPSIMD_NODES = slice(0, NODES // 4)
+SCALAR_NODES = slice(NODES // 4, NODES)
+MIX_ORDER = (0, 1, 2, 4, 3)
+SLOT = {0: 0, 1: 1, 2: 2, 4: 3, 3: 4}
 X1_NAMES = ("xa", "xb")
 
 FLOPS = 2 * 2 * BATCH * CHANNELS * NODES * NODES + 2 * BATCH * HIDDEN * NODES * GROUPS * CHANNELS
@@ -33,12 +35,14 @@ def tile_dcgrucell_pc_t_kernel(
     nc = tc.nc
     with ExitStack() as ctx:
         consts = ctx.enter_context(tc.tile_pool(name="consts", bufs=1))
-        rows_pool = ctx.enter_context(tc.tile_pool(name="rows", bufs=3))
-        gates_pool = ctx.enter_context(tc.tile_pool(name="gates", bufs=4))
+        rows_pool = ctx.enter_context(tc.tile_pool(name="rows", bufs=4))
+        gates_pool = ctx.enter_context(tc.tile_pool(name="gates", bufs=5))
+        nodes_pool = ctx.enter_context(tc.tile_pool(name="nodes", bufs=2))
+        group_pool = ctx.enter_context(tc.tile_pool(name="groups", bufs=3))
         work = ctx.enter_context(tc.tile_pool(name="work", bufs=2))
-        flip_pool = ctx.enter_context(tc.psum_pool(name="flip", bufs=2))
+        flip_pool = ctx.enter_context(tc.psum_pool(name="flip", bufs=3))
         diff_pool = ctx.enter_context(tc.psum_pool(name="diff", bufs=4))
-        mix_pool = ctx.enter_context(tc.psum_pool(name="mix", bufs=2))
+        mix_pool = ctx.enter_context(tc.psum_pool(name="mix", bufs=1))
         ctx.enter_context(tc.manual_schedule())
 
         x_sources = {"x0": x_cand, "xa": x1_0, "xb": x1_1}
@@ -46,17 +50,17 @@ def tile_dcgrucell_pc_t_kernel(
         loaded = {}
         by_node = {}
         flipped = {}
-        grouped = {}
+        pairs = {}
         h_mx = {}
         banks = {}
-        mixed = {}
         blend = {}
 
-        def load_rows(name, b):
+        def load_rows(name, b, parts=1):
             rows = rows_pool.tile([P, PACK, NODES], BF16, name=name)
-            nc.sync.dma_start(
-                out=rows[:], in_=x_sources[name][b].rearrange("(p j) n -> p j n", j=PACK)
-            )
+            source = x_sources[name][b].rearrange("(p j) n -> p j n", j=PACK)
+            step = PACK // parts
+            for j in range(0, PACK, step):
+                nc.sync.dma_start(out=rows[:, j : j + step, :], in_=source[:, j : j + step, :])
             loaded[(name, b)] = rows
 
         def load_gates(b):
@@ -70,51 +74,58 @@ def tile_dcgrucell_pc_t_kernel(
                 load_rows(name, b)
             load_gates(b)
 
-        def nodes_to_partitions(rows):
-            result = work.tile([P, PACK * P, PACK], BF16, name="by_node", align_bytes=64)
+        def flip_half(rows, result, half, copy):
             row_words = rows[:].bitcast(F32)
-            result_words = result[:].bitcast(F32)
-            for half in range(2):
-                bank = flip_pool.tile([P, 2, 2, P], F32, name="flip_bank")
-                for r in range(2):
-                    for v in range(2):
-                        nc.tensor.transpose(
-                            bank[:, r, v, :],
-                            row_words[:, 2 * half + r, v * P : (v + 1) * P],
-                            identity[:],
-                        )
-                nc.scalar.copy(
-                    out=result_words[:, 2 * P * half : 2 * P * (half + 1), :].rearrange(
-                        "q (r c) v -> q r c v", r=2
-                    ),
-                    in_=bank[:].rearrange("q r v c -> q r c v"),
-                )
-            return result
+            result_words = result.bitcast(F32)
+            bank = flip_pool.tile([P, 2, 2, P], F32, name="flip_bank")
+            for r in range(2):
+                for v in range(2):
+                    nc.tensor.transpose(
+                        bank[:, r, v, :],
+                        row_words[:, 2 * half + r, v * P : (v + 1) * P],
+                        identity[:],
+                    )
+            copy(
+                out=result_words[:, 2 * P * half : 2 * P * (half + 1), :].rearrange(
+                    "q (r c) v -> q r c v", r=2
+                ),
+                in_=bank[:].rearrange("q r v c -> q r c v"),
+            )
 
         def quantise(values, codes, scales):
             nc.vector.quantize_mx(
-                out=codes.bitcast(FP8X4),
-                scales=scales,
-                in_=values[:].rearrange("p c t -> p (c t)"),
+                out=codes.bitcast(FP8X4), scales=scales, in_=values.rearrange("p c t -> p (c t)")
             )
 
-        def flip(b, s):
-            by_node[(b, s)] = nodes_to_partitions(loaded[(X1_NAMES[s], b)])
+        def flip(b, s, half):
+            if b not in by_node:
+                by_node[b] = nodes_pool.tile(
+                    [P, 2 * CHANNELS, PACK], BF16, name="by_node", align_bytes=64
+                )
+            result = by_node[b][:, s * CHANNELS : (s + 1) * CHANNELS, :]
+            flip_half(loaded[(X1_NAMES[s], b)], result, half, nc.scalar.copy)
 
-        def quantise_flipped(b, s):
-            codes = work.tile([P, CHANNELS], U32, name="flip_codes%d" % s, align_bytes=64)
-            scales = work.tile([P, CHANNELS], U8, name="flip_scales%d" % s, align_bytes=64)
-            quantise(by_node[(b, s)], codes[:], scales[:])
-            flipped[(b, s)] = (codes, scales)
+        def quantise_flipped(b, graphs):
+            if (b, 0) not in flipped:
+                codes = work.tile([P, 2 * CHANNELS], U32, name="flip_codes", align_bytes=64)
+                scales = work.tile([P, 2 * CHANNELS], U8, name="flip_scales", align_bytes=64)
+                for s in range(2):
+                    part = slice(s * CHANNELS, (s + 1) * CHANNELS)
+                    flipped[(b, s)] = (codes[:, part], scales[:, part])
+                flipped[b] = (codes, scales)
+            codes, scales = flipped[b]
+            part = slice(graphs[0] * CHANNELS, (graphs[-1] + 1) * CHANNELS)
+            quantise(by_node[b][:, part, :], codes[:, part], scales[:, part])
 
         def group_tile(group, b):
-            if (group, b) not in grouped:
-                grouped[(group, b)] = work.tile(
-                    [P, NODES, PACK], BF16, name="h%d" % group, align_bytes=64
+            pair = SLOT[group] // 2
+            if (pair, b) not in pairs:
+                pairs[(pair, b)] = group_pool.tile(
+                    [P, 2 if pair < 2 else 1, NODES, PACK], BF16, name="h%d" % pair, align_bytes=64
                 )
-            return grouped[(group, b)]
+            return pairs[(pair, b)][:, SLOT[group] % 2, :, :]
 
-        def regroup(name, group, b, copy, nodes):
+        def regroup(name, group, b, copy, nodes=ALL_NODES):
             copy(
                 out=group_tile(group, b)[:, nodes, :].rearrange("p (c i) j -> p c j i", i=4),
                 in_=loaded[(name, b)][:, :, nodes].rearrange("p j (c i) -> p c j i", i=4),
@@ -148,43 +159,76 @@ def tile_dcgrucell_pc_t_kernel(
                     )
                 banks[(b, s)].append(bank)
 
-        def finish_x2(b, s):
+        def finish_x2(b, s, node_blocks=range(NODES // P)):
             x2 = group_tile(2 + 2 * s, b)
-            for m, bank in enumerate(banks[(b, s)]):
+            x0 = group_tile(0, b)
+            for m in node_blocks:
                 nc.vector.scalar_tensor_tensor(
                     out=x2[:, m * P : (m + 1) * P, :],
-                    in0=bank[:].rearrange("p j m -> p m j"),
+                    in0=banks[(b, s)][m][:].rearrange("p j m -> p m j"),
                     scalar=2.0,
-                    in1=grouped[(0, b)][:, m * P : (m + 1) * P, :],
+                    in1=x0[:, m * P : (m + 1) * P, :],
                     op0=ALU.mult,
                     op1=ALU.subtract,
                 )
 
-        def open_mix(b):
-            h_codes = work.tile([P, GROUPS, NODES], U32, name="h_codes", align_bytes=64)
-            h_scales = work.tile([P, GROUPS, NODES], U8, name="h_scales", align_bytes=64)
-            h_mx[b] = (h_codes, h_scales)
-            mixed[b] = mix_pool.tile([P, NODES], F32, name="mix_bank")
-
-        def mix_groups(b, groups):
+        def quantise_groups(b, groups, nodes=ALL_NODES):
+            if b not in h_mx:
+                h_mx[b] = (
+                    work.tile([P, GROUPS, NODES], U32, name="h_codes", align_bytes=64),
+                    work.tile([P, GROUPS, NODES], U8, name="h_scales", align_bytes=64),
+                )
             h_codes, h_scales = h_mx[b]
-            for g in groups:
-                quantise(grouped[(g, b)], h_codes[:, g, :], h_scales[:, g, :])
-            for g in groups:
-                nc.tensor.matmul_mx(
-                    out=mixed[b][:],
-                    lhsT=w_words[:, g, :].bitcast(FP8X4),
-                    lhsT_scale=w_scales[:, g, :],
-                    rhs=h_codes[:, g, :].bitcast(FP8X4),
-                    rhs_scale=h_scales[:, g, :],
-                    start=(g == 0),
-                    stop=(g == GROUPS - 1),
+            if len(groups) == 2:
+                first = SLOT[groups[0]]
+                nc.vector.quantize_mx(
+                    out=h_codes[:, first : first + 2, :].rearrange("p g n -> p (g n)").bitcast(FP8X4),
+                    scales=h_scales[:, first : first + 2, :].rearrange("p g n -> p (g n)"),
+                    in_=pairs[(first // 2, b)][:].rearrange("p g n t -> p (g n t)"),
+                )
+            else:
+                slot = SLOT[groups[0]]
+                quantise(
+                    group_tile(groups[0], b)[:, nodes, :], h_codes[:, slot, nodes], h_scales[:, slot, nodes]
                 )
 
-        def candidate(b):
-            cand = work.tile([P, NODES], F32, name="cand")
-            nc.scalar.activation(out=cand[:], in_=mixed[b][:], func=TANH, bias=bias[:, 0:1], scale=1.0)
-            blend[("cand", b)] = cand
+        def mix(b, bank, groups, first, last, nodes=ALL_NODES):
+            h_codes, h_scales = h_mx[b]
+            for g in groups:
+                nc.tensor.matmul_mx(
+                    out=bank[:, nodes],
+                    lhsT=w_words[:, g, :].bitcast(FP8X4),
+                    lhsT_scale=w_scales[:, g, :],
+                    rhs=h_codes[:, SLOT[g], nodes].bitcast(FP8X4),
+                    rhs_scale=h_scales[:, SLOT[g], nodes],
+                    start=(g == first),
+                    stop=(g == last),
+                )
+
+        def candidate(b, bank, nodes=ALL_NODES):
+            if ("cand", b) not in blend:
+                blend[("cand", b)] = work.tile([P, NODES], F32, name="cand")
+            nc.scalar.activation(
+                out=blend[("cand", b)][:, nodes],
+                in_=bank[:, nodes],
+                func=TANH,
+                bias=bias[:, 0:1],
+                scale=1.0,
+            )
+
+        def blend_on_gpsimd(b):
+            change = work.tile([P, NODES], F32, name="change")
+            gated = work.tile([P, NODES], F32, name="gated")
+            state = work.tile([P, NODES], F32, name="state")
+            cand = blend[("cand", b)]
+            nc.gpsimd.tensor_tensor(
+                out=change[:], in0=loaded[("hx", b)][:], in1=cand[:], op=ALU.subtract
+            )
+            nc.gpsimd.tensor_tensor(
+                out=gated[:], in0=loaded[("u", b)][:], in1=change[:], op=ALU.mult
+            )
+            nc.gpsimd.tensor_tensor(out=state[:], in0=gated[:], in1=cand[:], op=ALU.add)
+            nc.sync.dma_start(out=out[b], in_=state[:])
 
         def keep_old_state(b):
             kept = work.tile([P, NODES], F32, name="kept")
@@ -193,31 +237,30 @@ def tile_dcgrucell_pc_t_kernel(
             )
             blend[("kept", b)] = kept
 
-        def weigh_candidate(b):
+        def blend_on_vector(b, nodes):
             weighed = work.tile([P, NODES], F32, name="weighed")
+            state = work.tile([P, NODES], F32, name="state")
             nc.vector.scalar_tensor_tensor(
-                out=weighed[:],
-                in0=loaded[("u", b)][:],
+                out=weighed[:, nodes],
+                in0=loaded[("u", b)][:, nodes],
                 scalar=1.0,
-                in1=blend[("cand", b)][:],
+                in1=blend[("cand", b)][:, nodes],
                 op0=ALU.subtract,
                 op1=ALU.mult,
             )
-            blend[("weighed", b)] = weighed
-
-        def store_state(b, engine):
-            state = work.tile([P, NODES], F32, name="state")
-            engine.tensor_tensor(
-                out=state[:], in0=blend[("kept", b)][:], in1=blend[("weighed", b)][:], op=ALU.subtract
+            nc.vector.tensor_tensor(
+                out=state[:, nodes],
+                in0=blend[("kept", b)][:, nodes],
+                in1=weighed[:, nodes],
+                op=ALU.subtract,
             )
-            nc.sync.dma_start(out=out[b], in_=state[:])
+            nc.sync.dma_start(out=out[b][:, nodes], in_=state[:, nodes])
 
         identity = consts.tile([P, P], F32, name="identity")
         make_identity(nc, identity[:])
         w_words = consts.tile([P, GROUPS, HIDDEN], U32, name="w_words", align_bytes=64)
         w_scales = consts.tile([P, GROUPS, HIDDEN], U8, name="w_scales", align_bytes=64)
-        bias_rows = consts.tile([P, P], BF16, name="bias_rows")
-        nc.vector.memset(bias_rows[:], 0.0)
+        bias = consts.tile([P, 1], BF16, name="bias")
         nc.vector.memset(w_scales[:].bitcast(I32), 0)
 
         support_rows = []
@@ -229,8 +272,7 @@ def tile_dcgrucell_pc_t_kernel(
                 out=support_rows[s][:], in_=support.rearrange("(r p) n -> p r n", p=P)
             )
 
-        nc.sync.dma_start(out=bias_rows[0:1, :], in_=b_c.rearrange("(o h) -> o h", o=1))
-        load_rows("xa", 0)
+        load_rows("xa", 0, parts=2)
         load_support(0, support0)
         load_rows("x0", 0)
         load_rows("xb", 0)
@@ -246,69 +288,91 @@ def tile_dcgrucell_pc_t_kernel(
             )
         for name in ("xa", "xb", "x0"):
             load_rows(name, 1)
+        nc.sync.dma_start(out=bias[:], in_=b_c.rearrange("(h o) -> h o", o=1))
         load_gates(0)
         load_gates(1)
+        load_batch(2)
 
-        bias_rows_f32 = consts.tile([P, P], F32, name="bias_rows_f32")
-        nc.vector.tensor_copy(out=bias_rows_f32[:], in_=bias_rows[:])
-        bias_bank = flip_pool.tile([P, 2, 2, P], F32, name="flip_bank")
-        nc.tensor.transpose(bias_bank[:, 0, 0, :], bias_rows_f32[:], identity[:])
-        bias = consts.tile([P, 1], F32, name="bias")
-        nc.vector.tensor_copy(out=bias[:], in_=bias_bank[:, 0, 0, 0:1])
-
-        support_by_node = {}
         support_mx = {}
 
         def flip_support(s):
-            support_by_node[s] = nodes_to_partitions(support_rows[s])
+            result = consts.tile([P, NODES, PACK], BF16, name="support_by_node%d" % s, align_bytes=64)
+            for half in range(2):
+                flip_half(support_rows[s], result[:], half, nc.scalar.copy)
+            support_mx[s] = (
+                consts.tile([P, NODES], U32, name="support_codes%d" % s, align_bytes=64),
+                consts.tile([P, NODES], U8, name="support_scales%d" % s, align_bytes=64),
+            )
+            return result
 
-        def quantise_support(s):
-            codes = consts.tile([P, NODES], U32, name="support_codes%d" % s, align_bytes=64)
-            scales = consts.tile([P, NODES], U8, name="support_scales%d" % s, align_bytes=64)
-            quantise(support_by_node[s], codes[:], scales[:])
-            support_mx[s] = (codes, scales)
+        def quantise_support(s, result):
+            quantise(result[:], support_mx[s][0][:], support_mx[s][1][:])
 
-        regroup("xa", 1, 0, nc.vector.tensor_copy, ALL_NODES)
-        flip(0, 0)
-        flip_support(0)
-        quantise_flipped(0, 0)
-        regroup("x0", 0, 0, nc.vector.tensor_copy, ALL_NODES)
-        quantise_support(0)
+        flip(0, 0, 0)
+        flip(0, 0, 1)
+        support_by_node0 = flip_support(0)
+        regroup("xa", 1, 0, nc.vector.tensor_copy)
+        quantise_groups(0, (1,))
+        quantise_flipped(0, (0,))
+        quantise_support(0, support_by_node0)
+        regroup("x0", 0, 0, nc.scalar.copy)
+        flip(0, 1, 0)
+        flip(0, 1, 1)
         diffuse(0, 0)
+        support_by_node1 = flip_support(1)
+        regroup("xb", 3, 0, nc.vector.tensor_copy)
+        quantise_groups(0, (3,))
+        regroup_on_gpsimd("xb", 3, 1, GPSIMD_NODES)
         finish_x2(0, 0)
-        flip(0, 1)
-        flip_support(1)
-        quantise_flipped(0, 1)
-        quantise_support(1)
-        regroup("xb", 3, 0, nc.scalar.copy, ALL_NODES)
+        quantise_flipped(0, (1,))
+        quantise_support(1, support_by_node1)
+        quantise_groups(0, (0,))
+        quantise_groups(0, (2,))
 
-        for b in range(BATCH):
-            if b + 2 < BATCH:
-                load_batch(b + 2)
+        for b in range(BATCH - 1):
+            if b + 3 < BATCH:
+                load_batch(b + 3)
+            flip(b + 1, 0, 0)
+            flip(b + 1, 0, 1)
+            flip(b + 1, 1, 0)
             diffuse(b, 1)
-            if b + 1 < BATCH:
-                regroup("x0", 0, b + 1, nc.scalar.copy, ALL_NODES)
-                flip(b + 1, 0)
-                flip(b + 1, 1)
-            if b > 0:
-                candidate(b - 1)
-            if b + 1 < BATCH:
-                regroup("xa", 1, b + 1, nc.scalar.copy, ALL_NODES)
-                regroup("xb", 3, b + 1, nc.scalar.copy, SCALAR_NODES)
+            flip(b + 1, 1, 1)
+            regroup("x0", 0, b + 1, nc.scalar.copy)
+            regroup("xa", 1, b + 1, nc.scalar.copy)
+            regroup("xb", 3, b + 1, nc.scalar.copy, SCALAR_NODES)
+            bank = mix_pool.tile([P, NODES], F32, name="mix_bank")
             finish_x2(b, 1)
-            open_mix(b)
-            mix_groups(b, range(GROUPS))
-            if b + 1 < BATCH:
-                quantise_flipped(b + 1, 0)
-                quantise_flipped(b + 1, 1)
-                diffuse(b + 1, 0)
-            if b > 0:
-                weigh_candidate(b - 1)
-                store_state(b - 1, nc.gpsimd)
-            keep_old_state(b)
-            if b + 1 < BATCH:
-                regroup_on_gpsimd("xb", 3, b + 1, GPSIMD_NODES)
-                finish_x2(b + 1, 0)
-        candidate(BATCH - 1)
-        weigh_candidate(BATCH - 1)
-        store_state(BATCH - 1, nc.vector)
+            quantise_flipped(b + 1, (0, 1))
+            diffuse(b + 1, 0)
+            if b == 0:
+                quantise_groups(b, (4,))
+            else:
+                quantise_groups(b, (0, 1))
+                quantise_groups(b, (2, 4))
+                quantise_groups(b, (3,))
+            mix(b, bank, MIX_ORDER, MIX_ORDER[0], MIX_ORDER[-1])
+            candidate(b, bank)
+            blend_on_gpsimd(b)
+            if b + 2 < BATCH:
+                regroup_on_gpsimd("xb", 3, b + 2, GPSIMD_NODES)
+            finish_x2(b + 1, 0)
+
+        b = BATCH - 1
+        diffuse(b, 1)
+        keep_old_state(b)
+        pieces = [slice(0, 256), slice(256, 384), slice(384, 512)]
+        piece_banks = [mix_pool.tile([P, NODES], F32, name="mix_bank")]
+        for piece in pieces[1:]:
+            piece_banks.append(flip_pool.tile([P, NODES], F32, name="flip_bank"))
+        quantise_groups(b, (0, 1))
+        quantise_groups(b, (2,))
+        quantise_groups(b, (3,))
+        for piece, bank in zip(pieces, piece_banks):
+            mix(b, bank, (0, 1, 2, 3), 0, 4, piece)
+        for piece, bank in zip(pieces, piece_banks):
+            finish_x2(b, 1, range(piece.start // P, piece.stop // P))
+            quantise_groups(b, (4,), piece)
+            mix(b, bank, (4,), 0, 4, piece)
+            candidate(b, bank, piece)
+        for piece in pieces:
+            blend_on_vector(b, piece)

@@ -22,7 +22,7 @@ HIDDEN = 128
 ALL_NODES = slice(0, NODES)
 GPSIMD_NODES = slice(0, NODES // 4)
 SCALAR_NODES = slice(NODES // 4, NODES)
-MIX_ORDER = (0, 1, 2, 4, 3)
+MIX_ORDER = (0, 1, 3, 2, 4)
 SLOT = {0: 0, 1: 1, 2: 2, 4: 3, 3: 4}
 X1_NAMES = ("xa", "xb")
 
@@ -192,7 +192,7 @@ def tile_dcgrucell_pc_t_kernel(
                     group_tile(groups[0], b)[:, nodes, :], h_codes[:, slot, nodes], h_scales[:, slot, nodes]
                 )
 
-        def mix(b, bank, groups, first, last, nodes=ALL_NODES):
+        def mix(b, bank, groups, nodes=ALL_NODES):
             h_codes, h_scales = h_mx[b]
             for g in groups:
                 nc.tensor.matmul_mx(
@@ -201,8 +201,8 @@ def tile_dcgrucell_pc_t_kernel(
                     lhsT_scale=w_scales[:, g, :],
                     rhs=h_codes[:, SLOT[g], nodes].bitcast(FP8X4),
                     rhs_scale=h_scales[:, SLOT[g], nodes],
-                    start=(g == first),
-                    stop=(g == last),
+                    start=(g == MIX_ORDER[0]),
+                    stop=(g == MIX_ORDER[-1]),
                 )
 
         def candidate(b, bank, nodes=ALL_NODES):
@@ -238,8 +238,8 @@ def tile_dcgrucell_pc_t_kernel(
             blend[("kept", b)] = kept
 
         def blend_on_vector(b, nodes):
-            weighed = work.tile([P, NODES], F32, name="weighed")
-            state = work.tile([P, NODES], F32, name="state")
+            weighed = blend[("weighed", b)]
+            state = blend[("state", b)]
             nc.vector.scalar_tensor_tensor(
                 out=weighed[:, nodes],
                 in0=loaded[("u", b)][:, nodes],
@@ -326,31 +326,40 @@ def tile_dcgrucell_pc_t_kernel(
         finish_x2(0, 0)
         quantise_flipped(0, (1,))
         quantise_support(1, support_by_node1)
+        for s in range(2):
+            for half in range(2):
+                flip(1, s, half)
         quantise_groups(0, (0,))
         quantise_groups(0, (2,))
 
         for b in range(BATCH - 1):
             if b + 3 < BATCH:
                 load_batch(b + 3)
-            flip(b + 1, 0, 0)
-            flip(b + 1, 0, 1)
-            flip(b + 1, 1, 0)
-            diffuse(b, 1)
-            flip(b + 1, 1, 1)
+            if b == 0:
+                diffuse(b, 1)
+            else:
+                flip(b + 1, 0, 0)
+                flip(b + 1, 0, 1)
+                flip(b + 1, 1, 0)
+                diffuse(b, 1)
+                flip(b + 1, 1, 1)
             regroup("x0", 0, b + 1, nc.scalar.copy)
             regroup("xa", 1, b + 1, nc.scalar.copy)
             regroup("xb", 3, b + 1, nc.scalar.copy, SCALAR_NODES)
             bank = mix_pool.tile([P, NODES], F32, name="mix_bank")
+            if b == 0:
+                mix(b, bank, MIX_ORDER[:4])
             finish_x2(b, 1)
             quantise_flipped(b + 1, (0, 1))
             diffuse(b + 1, 0)
             if b == 0:
                 quantise_groups(b, (4,))
+                mix(b, bank, MIX_ORDER[4:])
             else:
                 quantise_groups(b, (0, 1))
-                quantise_groups(b, (2, 4))
                 quantise_groups(b, (3,))
-            mix(b, bank, MIX_ORDER, MIX_ORDER[0], MIX_ORDER[-1])
+                quantise_groups(b, (2, 4))
+                mix(b, bank, MIX_ORDER)
             candidate(b, bank)
             blend_on_gpsimd(b)
             if b + 2 < BATCH:
@@ -368,11 +377,13 @@ def tile_dcgrucell_pc_t_kernel(
         quantise_groups(b, (2,))
         quantise_groups(b, (3,))
         for piece, bank in zip(pieces, piece_banks):
-            mix(b, bank, (0, 1, 2, 3), 0, 4, piece)
+            mix(b, bank, MIX_ORDER[:4], piece)
         for piece, bank in zip(pieces, piece_banks):
             finish_x2(b, 1, range(piece.start // P, piece.stop // P))
             quantise_groups(b, (4,), piece)
-            mix(b, bank, (4,), 0, 4, piece)
+            mix(b, bank, MIX_ORDER[4:], piece)
             candidate(b, bank, piece)
+        blend[("weighed", b)] = work.tile([P, NODES], F32, name="weighed")
+        blend[("state", b)] = work.tile([P, NODES], F32, name="state")
         for piece in pieces:
             blend_on_vector(b, piece)

from contextlib import ExitStack

import concourse.mybir as mybir
from concourse.masks import make_identity

F32 = mybir.dt.float32
BF16 = mybir.dt.bfloat16
I32 = mybir.dt.int32
U32 = mybir.dt.uint32
U8 = mybir.dt.uint8
FP8X4 = mybir.dt.float8_e4m3fn_x4
ALU = mybir.AluOpType
TANH = mybir.ActivationFunctionType.Tanh

P = 128
PACK = 4
BATCH = 8
CHANNELS = 512
NODES = 512
GROUPS = 5
HIDDEN = 128
ALL_NODES = slice(0, NODES)
GPSIMD_NODES = slice(0, NODES // 4)
SCALAR_NODES = slice(NODES // 4, NODES)
MIX_ORDER = (0, 1, 3, 2, 4)
SLOT = {0: 0, 1: 1, 2: 2, 4: 3, 3: 4}
X1_NAMES = ("xa", "xb")

FLOPS = 2 * 2 * BATCH * CHANNELS * NODES * NODES + 2 * BATCH * HIDDEN * NODES * GROUPS * CHANNELS


def tile_dcgrucell_pc_t_kernel(
    tc, x_cand, x1_0, x1_1, support0, support1, W_c_words, W_c_scales, b_c, u, hx, out
):
    nc = tc.nc
    with ExitStack() as ctx:
        consts = ctx.enter_context(tc.tile_pool(name="consts", bufs=1))
        rows_pool = ctx.enter_context(tc.tile_pool(name="rows", bufs=4))
        gates_pool = ctx.enter_context(tc.tile_pool(name="gates", bufs=5))
        nodes_pool = ctx.enter_context(tc.tile_pool(name="nodes", bufs=2))
        group_pool = ctx.enter_context(tc.tile_pool(name="groups", bufs=3))
        work = ctx.enter_context(tc.tile_pool(name="work", bufs=2))
        flip_pool = ctx.enter_context(tc.psum_pool(name="flip", bufs=3))
        diff_pool = ctx.enter_context(tc.psum_pool(name="diff", bufs=4))
        mix_pool = ctx.enter_context(tc.psum_pool(name="mix", bufs=1))
        ctx.enter_context(tc.manual_schedule())

        x_sources = {"x0": x_cand, "xa": x1_0, "xb": x1_1}
        gate_sources = {"u": u, "hx": hx}
        loaded = {}
        by_node = {}
        flipped = {}
        pairs = {}
        h_mx = {}
        banks = {}
        blend = {}

        def load_rows(name, b, parts=1):
            rows = rows_pool.tile([P, PACK, NODES], BF16, name=name)
            source = x_sources[name][b].rearrange("(p j) n -> p j n", j=PACK)
            step = PACK // parts
            for j in range(0, PACK, step):
                nc.sync.dma_start(out=rows[:, j : j + step, :], in_=source[:, j : j + step, :])
            loaded[(name, b)] = rows

        def load_gates(b):
            for name in ("u", "hx"):
                gate = gates_pool.tile([P, NODES], BF16, name=name)
                nc.sync.dma_start(out=gate[:], in_=gate_sources[name][b])
                loaded[(name, b)] = gate

        def load_batch(b):
            for name in ("xa", "xb", "x0"):
                load_rows(name, b)
            load_gates(b)

        def flip_half(rows, result, half, copy):
            row_words = rows[:].bitcast(F32)
            result_words = result.bitcast(F32)
            bank = flip_pool.tile([P, 2, 2, P], F32, name="flip_bank")
            for r in range(2):
                for v in range(2):
                    nc.tensor.transpose(
                        bank[:, r, v, :],
                        row_words[:, 2 * half + r, v * P : (v + 1) * P],
                        identity[:],
                    )
            copy(
                out=result_words[:, 2 * P * half : 2 * P * (half + 1), :].rearrange(
                    "q (r c) v -> q r c v", r=2
                ),
                in_=bank[:].rearrange("q r v c -> q r c v"),
            )

        def quantise(values, codes, scales):
            nc.vector.quantize_mx(
                out=codes.bitcast(FP8X4), scales=scales, in_=values.rearrange("p c t -> p (c t)")
            )

        def flip(b, s, half):
            if b not in by_node:
                by_node[b] = nodes_pool.tile(
                    [P, 2 * CHANNELS, PACK], BF16, name="by_node", align_bytes=64
                )
            result = by_node[b][:, s * CHANNELS : (s + 1) * CHANNELS, :]
            flip_half(loaded[(X1_NAMES[s], b)], result, half, nc.scalar.copy)

        def quantise_flipped(b, graphs):
            if (b, 0) not in flipped:
                codes = work.tile([P, 2 * CHANNELS], U32, name="flip_codes", align_bytes=64)
                scales = work.tile([P, 2 * CHANNELS], U8, name="flip_scales", align_bytes=64)
                for s in range(2):
                    part = slice(s * CHANNELS, (s + 1) * CHANNELS)
                    flipped[(b, s)] = (codes[:, part], scales[:, part])
                flipped[b] = (codes, scales)
            codes, scales = flipped[b]
            part = slice(graphs[0] * CHANNELS, (graphs[-1] + 1) * CHANNELS)
            quantise(by_node[b][:, part, :], codes[:, part], scales[:, part])

        def group_tile(group, b):
            pair = SLOT[group] // 2
            if (pair, b) not in pairs:
                pairs[(pair, b)] = group_pool.tile(
                    [P, 2 if pair < 2 else 1, NODES, PACK], BF16, name="h%d" % pair, align_bytes=64
                )
            return pairs[(pair, b)][:, SLOT[group] % 2, :, :]

        def regroup(name, group, b, copy, nodes=ALL_NODES):
            copy(
                out=group_tile(group, b)[:, nodes, :].rearrange("p (c i) j -> p c j i", i=4),
                in_=loaded[(name, b)][:, :, nodes].rearrange("p j (c i) -> p c j i", i=4),
            )

        def regroup_on_gpsimd(name, group, b, nodes):
            nc.gpsimd.tensor_scalar(
                out=group_tile(group, b)[:, nodes, :],
                in0=loaded[(name, b)][:, :, nodes].rearrange("p j n -> p n j"),
                scalar1=1.0,
                scalar2=0.0,
                op0=ALU.mult,
                op1=ALU.add,
            )

        def diffuse(b, s):
            codes, scales = flipped[(b, s)]
            support_codes, support_scales = support_mx[s]
            banks[(b, s)] = []
            for m in range(NODES // P):
                bank = diff_pool.tile([P, PACK, P], F32, name="diff_bank")
                for j in range(PACK):
                    nc.tensor.matmul_mx(
                        out=bank[:, j, :],
                        lhsT=codes[:, j * P : (j + 1) * P].bitcast(FP8X4),
                        lhsT_scale=scales[:, j * P : (j + 1) * P],
                        rhs=support_codes[:, m * P : (m + 1) * P].bitcast(FP8X4),
                        rhs_scale=support_scales[:, m * P : (m + 1) * P],
                        start=True,
                        stop=True,
                    )
                banks[(b, s)].append(bank)

        def finish_x2(b, s, node_blocks=range(NODES // P)):
            x2 = group_tile(2 + 2 * s, b)
            x0 = group_tile(0, b)
            for m in node_blocks:
                nc.vector.scalar_tensor_tensor(
                    out=x2[:, m * P : (m + 1) * P, :],
                    in0=banks[(b, s)][m][:].rearrange("p j m -> p m j"),
                    scalar=2.0,
                    in1=x0[:, m * P : (m + 1) * P, :],
                    op0=ALU.mult,
                    op1=ALU.subtract,
                )

        def quantise_groups(b, groups, nodes=ALL_NODES):
            if b not in h_mx:
                h_mx[b] = (
                    work.tile([P, GROUPS, NODES], U32, name="h_codes", align_bytes=64),
                    work.tile([P, GROUPS, NODES], U8, name="h_scales", align_bytes=64),
                )
            h_codes, h_scales = h_mx[b]
            if len(groups) == 2:
                first = SLOT[groups[0]]
                nc.vector.quantize_mx(
                    out=h_codes[:, first : first + 2, :].rearrange("p g n -> p (g n)").bitcast(FP8X4),
                    scales=h_scales[:, first : first + 2, :].rearrange("p g n -> p (g n)"),
                    in_=pairs[(first // 2, b)][:].rearrange("p g n t -> p (g n t)"),
                )
            else:
                slot = SLOT[groups[0]]
                quantise(
                    group_tile(groups[0], b)[:, nodes, :], h_codes[:, slot, nodes], h_scales[:, slot, nodes]
                )

        def mix(b, bank, groups, nodes=ALL_NODES):
            h_codes, h_scales = h_mx[b]
            for g in groups:
                nc.tensor.matmul_mx(
                    out=bank[:, nodes],
                    lhsT=w_words[:, g, :].bitcast(FP8X4),
                    lhsT_scale=w_scales[:, g, :],
                    rhs=h_codes[:, SLOT[g], nodes].bitcast(FP8X4),
                    rhs_scale=h_scales[:, SLOT[g], nodes],
                    start=(g == MIX_ORDER[0]),
                    stop=(g == MIX_ORDER[-1]),
                )

        def candidate(b, bank, nodes=ALL_NODES):
            if ("cand", b) not in blend:
                blend[("cand", b)] = work.tile([P, NODES], F32, name="cand")
            nc.scalar.activation(
                out=blend[("cand", b)][:, nodes],
                in_=bank[:, nodes],
                func=TANH,
                bias=bias[:, 0:1],
                scale=1.0,
            )

        def blend_on_gpsimd(b):
            change = work.tile([P, NODES], F32, name="change")
            gated = work.tile([P, NODES], F32, name="gated")
            state = work.tile([P, NODES], F32, name="state")
            cand = blend[("cand", b)]
            nc.gpsimd.tensor_tensor(
                out=change[:], in0=loaded[("hx", b)][:], in1=cand[:], op=ALU.subtract
            )
            nc.gpsimd.tensor_tensor(
                out=gated[:], in0=loaded[("u", b)][:], in1=change[:], op=ALU.mult
            )
            nc.gpsimd.tensor_tensor(out=state[:], in0=gated[:], in1=cand[:], op=ALU.add)
            nc.sync.dma_start(out=out[b], in_=state[:])

        def keep_old_state(b):
            kept = work.tile([P, NODES], F32, name="kept")
            nc.gpsimd.tensor_tensor(
                out=kept[:], in0=loaded[("u", b)][:], in1=loaded[("hx", b)][:], op=ALU.mult
            )
            blend[("kept", b)] = kept

        def blend_on_vector(b, nodes):
            weighed = blend[("weighed", b)]
            state = blend[("state", b)]
            nc.vector.scalar_tensor_tensor(
                out=weighed[:, nodes],
                in0=loaded[("u", b)][:, nodes],
                scalar=1.0,
                in1=blend[("cand", b)][:, nodes],
                op0=ALU.subtract,
                op1=ALU.mult,
            )
            nc.vector.tensor_tensor(
                out=state[:, nodes],
                in0=blend[("kept", b)][:, nodes],
                in1=weighed[:, nodes],
                op=ALU.subtract,
            )
            nc.sync.dma_start(out=out[b][:, nodes], in_=state[:, nodes])

        identity = consts.tile([P, P], F32, name="identity")
        make_identity(nc, identity[:])
        w_words = consts.tile([P, GROUPS, HIDDEN], U32, name="w_words", align_bytes=64)
        w_scales = consts.tile([P, GROUPS, HIDDEN], U8, name="w_scales", align_bytes=64)
        bias = consts.tile([P, 1], BF16, name="bias")
        nc.vector.memset(w_scales[:].bitcast(I32), 0)

        support_rows = []
        for s in range(2):
            support_rows.append(consts.tile([P, PACK, NODES], BF16, name="support_rows%d" % s))

        def load_support(s, support):
            nc.sync.dma_start(
                out=support_rows[s][:], in_=support.rearrange("(r p) n -> p r n", p=P)
            )

        load_rows("xa", 0, parts=2)
        load_support(0, support0)
        load_rows("x0", 0)
        load_rows("xb", 0)
        load_support(1, support1)
        nc.sync.dma_start(
            out=w_words[:].bitcast(I32),
            in_=W_c_words.rearrange("g p n t -> p g (n t)").bitcast(I32),
        )
        scale_rows = W_c_scales.rearrange("g (q r) n -> r q g n", r=4)
        for r in range(4):
            nc.sync.dma_start(
                out=w_scales[r:P:32].bitcast(I32), in_=scale_rows[r].bitcast(I32)
            )
        for name in ("xa", "xb", "x0"):
            load_rows(name, 1)
        nc.sync.dma_start(out=bias[:], in_=b_c.rearrange("(h o) -> h o", o=1))
        load_gates(0)
        load_gates(1)
        load_batch(2)

        support_mx = {}

        def flip_support(s):
            result = consts.tile([P, NODES, PACK], BF16, name="support_by_node%d" % s, align_bytes=64)
            for half in range(2):
                flip_half(support_rows[s], result[:], half, nc.scalar.copy)
            support_mx[s] = (
                consts.tile([P, NODES], U32, name="support_codes%d" % s, align_bytes=64),
                consts.tile([P, NODES], U8, name="support_scales%d" % s, align_bytes=64),
            )
            return result

        def quantise_support(s, result):
            quantise(result[:], support_mx[s][0][:], support_mx[s][1][:])

        flip(0, 0, 0)
        flip(0, 0, 1)
        support_by_node0 = flip_support(0)
        regroup("xa", 1, 0, nc.vector.tensor_copy)
        quantise_groups(0, (1,))
        quantise_flipped(0, (0,))
        quantise_support(0, support_by_node0)
        regroup("x0", 0, 0, nc.scalar.copy)
        flip(0, 1, 0)
        flip(0, 1, 1)
        diffuse(0, 0)
        support_by_node1 = flip_support(1)
        regroup("xb", 3, 0, nc.vector.tensor_copy)
        quantise_groups(0, (3,))
        regroup_on_gpsimd("xb", 3, 1, GPSIMD_NODES)
        finish_x2(0, 0)
        quantise_flipped(0, (1,))
        quantise_support(1, support_by_node1)
        for s in range(2):
            for half in range(2):
                flip(1, s, half)
        quantise_groups(0, (0,))
        quantise_groups(0, (2,))

        for b in range(BATCH - 1):
            if b + 3 < BATCH:
                load_batch(b + 3)
            if b == 0:
                diffuse(b, 1)
            else:
                flip(b + 1, 0, 0)
                flip(b + 1, 0, 1)
                flip(b + 1, 1, 0)
                diffuse(b, 1)
                flip(b + 1, 1, 1)
            regroup("x0", 0, b + 1, nc.scalar.copy)
            regroup("xa", 1, b + 1, nc.scalar.copy)
            regroup("xb", 3, b + 1, nc.scalar.copy, SCALAR_NODES)
            bank = mix_pool.tile([P, NODES], F32, name="mix_bank")
            if b == 0:
                mix(b, bank, MIX_ORDER[:4])
            finish_x2(b, 1)
            quantise_flipped(b + 1, (0, 1))
            diffuse(b + 1, 0)
            if b == 0:
                quantise_groups(b, (4,))
                mix(b, bank, MIX_ORDER[4:])
            else:
                quantise_groups(b, (0, 1))
                quantise_groups(b, (3,))
                quantise_groups(b, (2, 4))
                mix(b, bank, MIX_ORDER)
            candidate(b, bank)
            blend_on_gpsimd(b)
            if b + 2 < BATCH:
                regroup_on_gpsimd("xb", 3, b + 2, GPSIMD_NODES)
            finish_x2(b + 1, 0)

        b = BATCH - 1
        diffuse(b, 1)
        keep_old_state(b)
        pieces = [slice(0, 256), slice(256, 384), slice(384, 512)]
        piece_banks = [mix_pool.tile([P, NODES], F32, name="mix_bank")]
        for piece in pieces[1:]:
            piece_banks.append(flip_pool.tile([P, NODES], F32, name="flip_bank"))
        quantise_groups(b, (0, 1))
        quantise_groups(b, (2,))
        quantise_groups(b, (3,))
        for piece, bank in zip(pieces, piece_banks):
            mix(b, bank, MIX_ORDER[:4], piece)
        for piece, bank in zip(pieces, piece_banks):
            finish_x2(b, 1, range(piece.start // P, piece.stop // P))
            quantise_groups(b, (4,), piece)
            mix(b, bank, MIX_ORDER[4:], piece)
            candidate(b, bank, piece)
        blend[("weighed", b)] = work.tile([P, NODES], F32, name="weighed")
        blend[("state", b)] = work.tile([P, NODES], F32, name="state")
        for piece in pieces:
            blend_on_vector(b, piece)
